import numpy as np
import ml_dtypes

BF16 = ml_dtypes.bfloat16


def bf(x):
    return np.asarray(x, np.float32).astype(BF16)


def f32(x):
    return np.asarray(x, np.float32)


def f64(x):
    return np.asarray(x).astype(np.float64)


def striped(idx):
    return np.tile(idx.reshape(-1, 16).T, (8, 1))


C, S, N = 256, 1024, 512
BASE = 10000.0


def pos_encoding():
    pos = np.arange(N, dtype=np.float32)[None, :]
    i = np.arange(C // 2, dtype=np.float32)[:, None]
    ang = pos / np.power(np.float32(BASE), np.float32(2.0) * i / np.float32(C))
    pe = np.zeros((C, N), np.float32)
    pe[0::2] = np.sin(ang)
    pe[1::2] = np.cos(ang)
    return pe


def setup_inputs():
    return {"emb": f32(np.random.standard_normal((C, S))), "pe": f32(pos_encoding()), "w_out": bf(np.random.standard_normal((C, S)) / np.sqrt(C)), "offs": striped(np.random.permutation(np.tile(np.arange(S), 2))[:N])}


def reference(emb, pe, w_out, offs):
    idx = offs[:16].T.reshape(-1)
    h = f64(emb)[:, idx] + f64(pe)
    return f64(w_out).T @ h

@@ -1,0 +1,55 @@
+import concourse.mybir as mybir
+
+P = 128
+C, S, N = 256, 1024, 512
+CB = C // P
+VB = S // P
+FLOPS = 2 * C * S * N
+
+F32, BF16, U16 = mybir.dt.float32, mybir.dt.bfloat16, mybir.dt.uint16
+ADD = mybir.AluOpType.add
+
+
+def tile_lumiere1m_kernel(tc, emb, pe, w_out, offs, out):
+    nc = tc.nc
+    with (
+        tc.tile_pool(name="held", bufs=1) as held,
+        tc.tile_pool(name="staging", bufs=4) as staging,
+        tc.psum_pool(name="psum", bufs=1) as psum,
+    ):
+        offsets = held.tile([P, N // 16], U16, name="offsets")
+        nc.sync.dma_start(offsets[:], offs)
+
+        table, place, weights = [], [], []
+        for cb in range(CB):
+            rows = slice(cb * P, (cb + 1) * P)
+            table.append(held.tile([P, S], F32, name=f"table{cb}"))
+            place.append(held.tile([P, N], F32, name=f"place{cb}"))
+            weights.append(held.tile([P, S], BF16, name=f"weights{cb}"))
+            nc.sync.dma_start(table[cb][:], emb[rows, :])
+            nc.sync.dma_start(place[cb][:], pe[rows, :])
+            nc.sync.dma_start(weights[cb][:], w_out[rows, :])
+
+        logits = [psum.tile([P, N], F32, name=f"logits{vb}") for vb in range(VB)]
+
+        for cb in range(CB):
+            hidden32 = held.tile([P, N], F32, name=f"hidden32_{cb}")
+            nc.vector.tensor_tensor(hidden32[:], table[cb][:].indirect(offsets[:]), place[cb][:], ADD)
+            hidden = held.tile([P, N], BF16, name=f"hidden{cb}")
+            nc.scalar.copy(hidden[:], hidden32[:])
+            for vb in range(VB):
+                nc.tensor.matmul(
+                    logits[vb][:],
+                    weights[cb][:, vb * P : (vb + 1) * P],
+                    hidden[:],
+                    start=(cb == 0),
+                    stop=(cb == CB - 1),
+                )
+
+        for vb in range(VB):
+            staged = staging.tile([P, N], F32, name="staged")
+            if vb % 2 == 0:
+                nc.vector.tensor_copy(staged[:], logits[vb][:])
+            else:
+                nc.scalar.copy(staged[:], logits[vb][:])
+            nc.sync.dma_start(out[vb * P : (vb + 1) * P, :], staged[:])

@@ -4,6 +4,8 @@ P = 128
 C, S, N = 256, 1024, 512
 CB = C // P
 VB = S // P
+PIECES = 2
+NP = N // PIECES
 FLOPS = 2 * C * S * N
 
 F32, BF16, U16 = mybir.dt.float32, mybir.dt.bfloat16, mybir.dt.uint16
@@ -14,8 +16,8 @@ def tile_lumiere1m_kernel(tc, emb, pe, w_out, offs, out):
     nc = tc.nc
     with (
         tc.tile_pool(name="held", bufs=1) as held,
-        tc.tile_pool(name="staging", bufs=4) as staging,
-        tc.psum_pool(name="psum", bufs=1) as psum,
+        tc.tile_pool(name="staging", bufs=PIECES * VB) as staging,
+        tc.psum_pool(name="psum", bufs=VB) as psum,
     ):
         offsets = held.tile([P, N // 16], U16, name="offsets")
         nc.sync.dma_start(offsets[:], offs)
@@ -30,26 +32,34 @@ def tile_lumiere1m_kernel(tc, emb, pe, w_out, offs, out):
             nc.sync.dma_start(place[cb][:], pe[rows, :])
             nc.sync.dma_start(weights[cb][:], w_out[rows, :])
 
-        logits = [psum.tile([P, N], F32, name=f"logits{vb}") for vb in range(VB)]
-
+        hidden = {}
         for cb in range(CB):
-            hidden32 = held.tile([P, N], F32, name=f"hidden32_{cb}")
-            nc.vector.tensor_tensor(hidden32[:], table[cb][:].indirect(offsets[:]), place[cb][:], ADD)
-            hidden = held.tile([P, N], BF16, name=f"hidden{cb}")
-            nc.scalar.copy(hidden[:], hidden32[:])
-            for vb in range(VB):
-                nc.tensor.matmul(
-                    logits[vb][:],
-                    weights[cb][:, vb * P : (vb + 1) * P],
-                    hidden[:],
-                    start=(cb == 0),
-                    stop=(cb == CB - 1),
+            for piece in range(PIECES):
+                hidden32 = held.tile([P, NP], F32, name=f"hidden32_{cb}_{piece}")
+                nc.vector.tensor_tensor(
+                    hidden32[:],
+                    table[cb][:].indirect(offsets[:, piece * (NP // 16) : (piece + 1) * (NP // 16)]),
+                    place[cb][:, piece * NP : (piece + 1) * NP],
+                    ADD,
                 )
+                hidden[cb, piece] = held.tile([P, NP], BF16, name=f"hidden_{cb}_{piece}")
+                nc.scalar.copy(hidden[cb, piece][:], hidden32[:])
 
-        for vb in range(VB):
-            staged = staging.tile([P, N], F32, name="staged")
-            if vb % 2 == 0:
-                nc.vector.tensor_copy(staged[:], logits[vb][:])
-            else:
-                nc.scalar.copy(staged[:], logits[vb][:])
-            nc.sync.dma_start(out[vb * P : (vb + 1) * P, :], staged[:])
+        for piece in range(PIECES):
+            logits = [psum.tile([P, NP], F32, name="logits") for vb in range(VB)]
+            for cb in range(CB):
+                for vb in range(VB):
+                    nc.tensor.matmul(
+                        logits[vb][:],
+                        weights[cb][:, vb * P : (vb + 1) * P],
+                        hidden[cb, piece][:],
+                        start=(cb == 0),
+                        stop=(cb == CB - 1),
+                    )
+            for vb in range(VB):
+                staged = staging.tile([P, NP], F32, name="staged")
+                if vb % 2 == 0:
+                    nc.vector.tensor_copy(staged[:], logits[vb][:])
+                else:
+                    nc.scalar.copy(staged[:], logits[vb][:])
+                nc.sync.dma_start(out[vb * P : (vb + 1) * P, piece * NP : (piece + 1) * NP], staged[:])

@@ -6,6 +6,7 @@ CB = C // P
 VB = S // P
 PIECES = 2
 NP = N // PIECES
+WARMUPS = 12
 FLOPS = 2 * C * S * N
 
 F32, BF16, U16 = mybir.dt.float32, mybir.dt.bfloat16, mybir.dt.uint16
@@ -31,6 +32,12 @@ def tile_lumiere1m_kernel(tc, emb, pe, w_out, offs, out):
             nc.sync.dma_start(table[cb][:], emb[rows, :])
             nc.sync.dma_start(place[cb][:], pe[rows, :])
             nc.sync.dma_start(weights[cb][:], w_out[rows, :])
+
+        zeros = held.tile([P, N], BF16, name="zeros")
+        nc.gpsimd.memset(zeros[:], 0.0)
+        unread = psum.tile([P, N], F32, name="unread", tag="logits")
+        for warmup in range(WARMUPS):
+            nc.tensor.matmul(unread[:], zeros[:, 0:P], zeros[:], start=True, stop=True)
 
         hidden = {}
         for cb in range(CB):

@@ -3,10 +3,12 @@ import concourse.mybir as mybir
 P = 128
 C, S, N = 256, 1024, 512
 CB = C // P
-VB = S // P
 PIECES = 2
 NP = N // PIECES
-WARMUPS = 12
+PARTS = 2
+SP = S // PARTS
+VB = SP // P
+WARMUPS = 10
 FLOPS = 2 * C * S * N
 
 F32, BF16, U16 = mybir.dt.float32, mybir.dt.bfloat16, mybir.dt.uint16
@@ -17,21 +19,32 @@ def tile_lumiere1m_kernel(tc, emb, pe, w_out, offs, out):
     nc = tc.nc
     with (
         tc.tile_pool(name="held", bufs=1) as held,
-        tc.tile_pool(name="staging", bufs=PIECES * VB) as staging,
-        tc.psum_pool(name="psum", bufs=VB) as psum,
+        tc.tile_pool(name="staging", bufs=PIECES * PARTS * VB) as staging,
+        tc.psum_pool(name="psum", bufs=8) as psum,
     ):
         offsets = held.tile([P, N // 16], U16, name="offsets")
         nc.sync.dma_start(offsets[:], offs)
 
-        table, place, weights = [], [], []
+        table = [held.tile([P, S], F32, name=f"table{cb}") for cb in range(CB)]
+        place = {(cb, piece): held.tile([P, NP], F32, name=f"place{cb}_{piece}")
+                 for cb in range(CB) for piece in range(PIECES)}
+        weights = {(cb, part): held.tile([P, SP], BF16, name=f"weights{cb}_{part}")
+                   for cb in range(CB) for part in range(PARTS)}
+
+        def load_place(piece):
+            for cb in range(CB):
+                nc.sync.dma_start(place[cb, piece][:], pe[cb * P : (cb + 1) * P, piece * NP : (piece + 1) * NP])
+
+        def load_weights(part):
+            for cb in range(CB):
+                nc.sync.dma_start(weights[cb, part][:], w_out[cb * P : (cb + 1) * P, part * SP : (part + 1) * SP])
+
         for cb in range(CB):
-            rows = slice(cb * P, (cb + 1) * P)
-            table.append(held.tile([P, S], F32, name=f"table{cb}"))
-            place.append(held.tile([P, N], F32, name=f"place{cb}"))
-            weights.append(held.tile([P, S], BF16, name=f"weights{cb}"))
-            nc.sync.dma_start(table[cb][:], emb[rows, :])
-            nc.sync.dma_start(place[cb][:], pe[rows, :])
-            nc.sync.dma_start(weights[cb][:], w_out[rows, :])
+            nc.sync.dma_start(table[cb][:], emb[cb * P : (cb + 1) * P, :])
+            nc.sync.dma_start(place[cb, 0][:], pe[cb * P : (cb + 1) * P, 0:NP])
+        load_weights(0)
+        load_place(1)
+        load_weights(1)
 
         zeros = held.tile([P, N], BF16, name="zeros")
         nc.gpsimd.memset(zeros[:], 0.0)
@@ -39,34 +52,35 @@ def tile_lumiere1m_kernel(tc, emb, pe, w_out, offs, out):
         for warmup in range(WARMUPS):
             nc.tensor.matmul(unread[:], zeros[:, 0:P], zeros[:], start=True, stop=True)
 
-        hidden = {}
-        for cb in range(CB):
-            for piece in range(PIECES):
+        for piece in range(PIECES):
+            hidden = []
+            for cb in range(CB):
                 hidden32 = held.tile([P, NP], F32, name=f"hidden32_{cb}_{piece}")
                 nc.vector.tensor_tensor(
                     hidden32[:],
                     table[cb][:].indirect(offsets[:, piece * (NP // 16) : (piece + 1) * (NP // 16)]),
-                    place[cb][:, piece * NP : (piece + 1) * NP],
+                    place[cb, piece][:],
                     ADD,
                 )
-                hidden[cb, piece] = held.tile([P, NP], BF16, name=f"hidden_{cb}_{piece}")
-                nc.scalar.copy(hidden[cb, piece][:], hidden32[:])
+                hidden.append(held.tile([P, NP], BF16, name=f"hidden{cb}_{piece}"))
+                nc.scalar.copy(hidden[cb][:], hidden32[:])
 
-        for piece in range(PIECES):
-            logits = [psum.tile([P, NP], F32, name="logits") for vb in range(VB)]
-            for cb in range(CB):
+            for part in range(PARTS):
+                logits = [psum.tile([P, NP], F32, name="logits") for vb in range(VB)]
+                for cb in range(CB):
+                    for vb in range(VB):
+                        nc.tensor.matmul(
+                            logits[vb][:],
+                            weights[cb, part][:, vb * P : (vb + 1) * P],
+                            hidden[cb][:],
+                            start=(cb == 0),
+                            stop=(cb == CB - 1),
+                        )
                 for vb in range(VB):
-                    nc.tensor.matmul(
-                        logits[vb][:],
-                        weights[cb][:, vb * P : (vb + 1) * P],
-                        hidden[cb, piece][:],
-                        start=(cb == 0),
-                        stop=(cb == CB - 1),
-                    )
-            for vb in range(VB):
-                staged = staging.tile([P, NP], F32, name="staged")
-                if vb % 2 == 0:
-                    nc.vector.tensor_copy(staged[:], logits[vb][:])
-                else:
-                    nc.scalar.copy(staged[:], logits[vb][:])
-                nc.sync.dma_start(out[vb * P : (vb + 1) * P, piece * NP : (piece + 1) * NP], staged[:])
+                    staged = staging.tile([P, NP], F32, name="staged")
+                    if vb % 2 == 0:
+                        nc.vector.tensor_copy(staged[:], logits[vb][:])
+                    else:
+                        nc.scalar.copy(staged[:], logits[vb][:])
+                    first_row = part * SP + vb * P
+                    nc.sync.dma_start(out[first_row : first_row + P, piece * NP : (piece + 1) * NP], staged[:])

@@ -42,8 +42,8 @@ def tile_lumiere1m_kernel(tc, emb, pe, w_out, offs, out):
         for cb in range(CB):
             nc.sync.dma_start(table[cb][:], emb[cb * P : (cb + 1) * P, :])
             nc.sync.dma_start(place[cb, 0][:], pe[cb * P : (cb + 1) * P, 0:NP])
-        load_weights(0)
         load_place(1)
+        load_weights(0)
         load_weights(1)
 
         zeros = held.tile([P, N], BF16, name="zeros")
@@ -52,8 +52,8 @@ def tile_lumiere1m_kernel(tc, emb, pe, w_out, offs, out):
         for warmup in range(WARMUPS):
             nc.tensor.matmul(unread[:], zeros[:, 0:P], zeros[:], start=True, stop=True)
 
+        hidden = {}
         for piece in range(PIECES):
-            hidden = []
             for cb in range(CB):
                 hidden32 = held.tile([P, NP], F32, name=f"hidden32_{cb}_{piece}")
                 nc.vector.tensor_tensor(
@@ -62,9 +62,10 @@ def tile_lumiere1m_kernel(tc, emb, pe, w_out, offs, out):
                     place[cb, piece][:],
                     ADD,
                 )
-                hidden.append(held.tile([P, NP], BF16, name=f"hidden{cb}_{piece}"))
-                nc.scalar.copy(hidden[cb][:], hidden32[:])
+                hidden[cb, piece] = held.tile([P, NP], BF16, name=f"hidden{cb}_{piece}")
+                nc.scalar.copy(hidden[cb, piece][:], hidden32[:])
 
+        for piece in range(PIECES):
             for part in range(PARTS):
                 logits = [psum.tile([P, NP], F32, name="logits") for vb in range(VB)]
                 for cb in range(CB):
@@ -72,7 +73,7 @@ def tile_lumiere1m_kernel(tc, emb, pe, w_out, offs, out):
                         nc.tensor.matmul(
                             logits[vb][:],
                             weights[cb, part][:, vb * P : (vb + 1) * P],
-                            hidden[cb][:],
+                            hidden[cb, piece][:],
                             start=(cb == 0),
                             stop=(cb == CB - 1),
                         )

@@ -19,7 +19,7 @@ def tile_lumiere1m_kernel(tc, emb, pe, w_out, offs, out):
     nc = tc.nc
     with (
         tc.tile_pool(name="held", bufs=1) as held,
-        tc.tile_pool(name="staging", bufs=PIECES * PARTS * VB) as staging,
+        tc.tile_pool(name="staging", bufs=PIECES * VB) as staging,
         tc.psum_pool(name="psum", bufs=8) as psum,
     ):
         offsets = held.tile([P, N // 16], U16, name="offsets")
@@ -65,23 +65,35 @@ def tile_lumiere1m_kernel(tc, emb, pe, w_out, offs, out):
                 hidden[cb, piece] = held.tile([P, NP], BF16, name=f"hidden{cb}_{piece}")
                 nc.scalar.copy(hidden[cb, piece][:], hidden32[:])
 
+        def project(blocks, piece):
+            logits = {vb: psum.tile([P, NP], F32, name="logits") for vb in blocks}
+            for cb in range(CB):
+                for vb in blocks:
+                    nc.tensor.matmul(
+                        logits[vb][:],
+                        weights[cb, vb // VB][:, (vb % VB) * P : (vb % VB + 1) * P],
+                        hidden[cb, piece][:],
+                        start=(cb == 0),
+                        stop=(cb == CB - 1),
+                    )
+            return logits
+
+        def evacuate(staged_columns, logits, turn):
+            if turn % 2 == 0:
+                nc.vector.tensor_copy(staged_columns, logits[:])
+            else:
+                nc.scalar.copy(staged_columns, logits[:])
+
         for piece in range(PIECES):
-            for part in range(PARTS):
-                logits = [psum.tile([P, NP], F32, name="logits") for vb in range(VB)]
-                for cb in range(CB):
-                    for vb in range(VB):
-                        nc.tensor.matmul(
-                            logits[vb][:],
-                            weights[cb, part][:, vb * P : (vb + 1) * P],
-                            hidden[cb, piece][:],
-                            start=(cb == 0),
-                            stop=(cb == CB - 1),
-                        )
-                for vb in range(VB):
-                    staged = staging.tile([P, NP], F32, name="staged")
-                    if vb % 2 == 0:
-                        nc.vector.tensor_copy(staged[:], logits[vb][:])
-                    else:
-                        nc.scalar.copy(staged[:], logits[vb][:])
-                    first_row = part * SP + vb * P
-                    nc.sync.dma_start(out[first_row : first_row + P, piece * NP : (piece + 1) * NP], staged[:])
+            logits = project(range(VB), piece)
+            for vb in range(VB):
+                staged = staging.tile([P, NP], F32, name="staged_half")
+                evacuate(staged[:], logits[vb], vb)
+                nc.sync.dma_start(out[vb * P : (vb + 1) * P, piece * NP : (piece + 1) * NP], staged[:])
+
+        for vb in range(VB, 2 * VB):
+            staged = staging.tile([P, N], F32, name="staged_whole")
+            for piece in range(PIECES):
+                logits = project([vb], piece)
+                evacuate(staged[:, piece * NP : (piece + 1) * NP], logits[vb], piece)
+            nc.sync.dma_start(out[vb * P : (vb + 1) * P, :], staged[:])

@@ -20,7 +20,7 @@ def tile_lumiere1m_kernel(tc, emb, pe, w_out, offs, out):
     with (
         tc.tile_pool(name="held", bufs=1) as held,
         tc.tile_pool(name="staging", bufs=PIECES * VB) as staging,
-        tc.psum_pool(name="psum", bufs=8) as psum,
+        tc.psum_pool(name="psum", bufs=VB) as psum,
     ):
         offsets = held.tile([P, N // 16], U16, name="offsets")
         nc.sync.dma_start(offsets[:], offs)
@@ -48,7 +48,7 @@ def tile_lumiere1m_kernel(tc, emb, pe, w_out, offs, out):
 
         zeros = held.tile([P, N], BF16, name="zeros")
         nc.gpsimd.memset(zeros[:], 0.0)
-        unread = psum.tile([P, N], F32, name="unread", tag="logits")
+        unread = psum.tile([P, N], F32, name="unread", tag="half_rows")
         for warmup in range(WARMUPS):
             nc.tensor.matmul(unread[:], zeros[:, 0:P], zeros[:], start=True, stop=True)
 
@@ -65,35 +65,36 @@ def tile_lumiere1m_kernel(tc, emb, pe, w_out, offs, out):
                 hidden[cb, piece] = held.tile([P, NP], BF16, name=f"hidden{cb}_{piece}")
                 nc.scalar.copy(hidden[cb, piece][:], hidden32[:])
 
-        def project(blocks, piece):
-            logits = {vb: psum.tile([P, NP], F32, name="logits") for vb in blocks}
-            for cb in range(CB):
-                for vb in blocks:
-                    nc.tensor.matmul(
-                        logits[vb][:],
-                        weights[cb, vb // VB][:, (vb % VB) * P : (vb % VB + 1) * P],
-                        hidden[cb, piece][:],
-                        start=(cb == 0),
-                        stop=(cb == CB - 1),
-                    )
-            return logits
+        def project(logits, vb, piece, cb):
+            nc.tensor.matmul(
+                logits,
+                weights[cb, vb // VB][:, (vb % VB) * P : (vb % VB + 1) * P],
+                hidden[cb, piece][:],
+                start=(cb == 0),
+                stop=(cb == CB - 1),
+            )
 
-        def evacuate(staged_columns, logits, turn):
-            if turn % 2 == 0:
-                nc.vector.tensor_copy(staged_columns, logits[:])
+        def evacuate(staged, logits, vb):
+            if vb % 2 == 0:
+                nc.vector.tensor_copy(staged[:], logits[:])
             else:
-                nc.scalar.copy(staged_columns, logits[:])
+                nc.scalar.copy(staged[:], logits[:])
 
         for piece in range(PIECES):
-            logits = project(range(VB), piece)
+            logits = [psum.tile([P, NP], F32, name="half_rows") for vb in range(VB)]
+            for cb in range(CB):
+                for vb in range(VB):
+                    project(logits[vb][:], vb, piece, cb)
             for vb in range(VB):
                 staged = staging.tile([P, NP], F32, name="staged_half")
-                evacuate(staged[:], logits[vb], vb)
+                evacuate(staged, logits[vb], vb)
                 nc.sync.dma_start(out[vb * P : (vb + 1) * P, piece * NP : (piece + 1) * NP], staged[:])
 
         for vb in range(VB, 2 * VB):
-            staged = staging.tile([P, N], F32, name="staged_whole")
+            logits = psum.tile([P, N], F32, name="whole_rows")
             for piece in range(PIECES):
-                logits = project([vb], piece)
-                evacuate(staged[:, piece * NP : (piece + 1) * NP], logits[vb], piece)
+                for cb in range(CB):
+                    project(logits[:, piece * NP : (piece + 1) * NP], vb, piece, cb)
+            staged = staging.tile([P, N], F32, name="staged_whole")
+            evacuate(staged, logits, vb)
             nc.sync.dma_start(out[vb * P : (vb + 1) * P, :], staged[:])

@@ -31,20 +31,20 @@ def tile_lumiere1m_kernel(tc, emb, pe, w_out, offs, out):
         weights = {(cb, part): held.tile([P, SP], BF16, name=f"weights{cb}_{part}")
                    for cb in range(CB) for part in range(PARTS)}
 
-        def load_place(piece):
-            for cb in range(CB):
-                nc.sync.dma_start(place[cb, piece][:], pe[cb * P : (cb + 1) * P, piece * NP : (piece + 1) * NP])
+        def load_place(cb, piece):
+            nc.sync.dma_start(place[cb, piece][:], pe[cb * P : (cb + 1) * P, piece * NP : (piece + 1) * NP])
 
-        def load_weights(part):
-            for cb in range(CB):
-                nc.sync.dma_start(weights[cb, part][:], w_out[cb * P : (cb + 1) * P, part * SP : (part + 1) * SP])
+        def load_weights(cb, part):
+            nc.sync.dma_start(weights[cb, part][:], w_out[cb * P : (cb + 1) * P, part * SP : (part + 1) * SP])
 
         for cb in range(CB):
             nc.sync.dma_start(table[cb][:], emb[cb * P : (cb + 1) * P, :])
-            nc.sync.dma_start(place[cb, 0][:], pe[cb * P : (cb + 1) * P, 0:NP])
-        load_place(1)
-        load_weights(0)
-        load_weights(1)
+            load_place(cb, 0)
+        for cb in range(CB):
+            load_place(cb, 1)
+            load_weights(cb, 0)
+        for cb in range(CB):
+            load_weights(cb, 1)
 
         zeros = held.tile([P, N], BF16, name="zeros")
         nc.gpsimd.memset(zeros[:], 0.0)

@@ -74,8 +74,8 @@ def tile_lumiere1m_kernel(tc, emb, pe, w_out, offs, out):
                 stop=(cb == CB - 1),
             )
 
-        def evacuate(staged, logits, vb):
-            if vb % 2 == 0:
+        def evacuate(staged, logits, by_vector):
+            if by_vector:
                 nc.vector.tensor_copy(staged[:], logits[:])
             else:
                 nc.scalar.copy(staged[:], logits[:])
@@ -87,7 +87,7 @@ def tile_lumiere1m_kernel(tc, emb, pe, w_out, offs, out):
                     project(logits[vb][:], vb, piece, cb)
             for vb in range(VB):
                 staged = staging.tile([P, NP], F32, name="staged_half")
-                evacuate(staged, logits[vb], vb)
+                evacuate(staged, logits[vb], by_vector=(vb < VB // 2))
                 nc.sync.dma_start(out[vb * P : (vb + 1) * P, piece * NP : (piece + 1) * NP], staged[:])
 
         for vb in range(VB, 2 * VB):
@@ -96,5 +96,5 @@ def tile_lumiere1m_kernel(tc, emb, pe, w_out, offs, out):
                 for cb in range(CB):
                     project(logits[:, piece * NP : (piece + 1) * NP], vb, piece, cb)
             staged = staging.tile([P, N], F32, name="staged_whole")
-            evacuate(staged, logits, vb)
+            evacuate(staged, logits, by_vector=(vb % 2 == 0))
             nc.sync.dma_start(out[vb * P : (vb + 1) * P, :], staged[:])

@@ -76,9 +76,9 @@ def tile_lumiere1m_kernel(tc, emb, pe, w_out, offs, out):
 
         def evacuate(staged, logits, by_vector):
             if by_vector:
-                nc.vector.tensor_copy(staged[:], logits[:])
+                nc.vector.tensor_copy(staged, logits)
             else:
-                nc.scalar.copy(staged[:], logits[:])
+                nc.scalar.copy(staged, logits)
 
         for piece in range(PIECES):
             logits = [psum.tile([P, NP], F32, name="half_rows") for vb in range(VB)]
@@ -87,14 +87,15 @@ def tile_lumiere1m_kernel(tc, emb, pe, w_out, offs, out):
                     project(logits[vb][:], vb, piece, cb)
             for vb in range(VB):
                 staged = staging.tile([P, NP], F32, name="staged_half")
-                evacuate(staged, logits[vb], by_vector=(vb < VB // 2))
+                evacuate(staged[:], logits[vb][:], by_vector=(vb < VB // 2))
                 nc.sync.dma_start(out[vb * P : (vb + 1) * P, piece * NP : (piece + 1) * NP], staged[:])
 
         for vb in range(VB, 2 * VB):
-            logits = psum.tile([P, N], F32, name="whole_rows")
-            for piece in range(PIECES):
-                for cb in range(CB):
-                    project(logits[:, piece * NP : (piece + 1) * NP], vb, piece, cb)
             staged = staging.tile([P, N], F32, name="staged_whole")
-            evacuate(staged, logits, by_vector=(vb % 2 == 0))
+            for piece in range(PIECES):
+                bank = psum.tile([P, N], F32, name="whole_rows")
+                logits = bank[:, 0:NP]
+                for cb in range(CB):
+                    project(logits, vb, piece, cb)
+                evacuate(staged[:, piece * NP : (piece + 1) * NP], logits, by_vector=(piece == 0))
             nc.sync.dma_start(out[vb * P : (vb + 1) * P, :], staged[:])

@@ -82,9 +82,11 @@ def tile_lumiere1m_kernel(tc, emb, pe, w_out, offs, out):
 
         for piece in range(PIECES):
             logits = [psum.tile([P, NP], F32, name="half_rows") for vb in range(VB)]
-            for cb in range(CB):
-                for vb in range(VB):
-                    project(logits[vb][:], vb, piece, cb)
+            steps = [(cb, vb) for cb in range(CB) for vb in range(VB)]
+            if piece > 0:
+                steps = [(cb, vb) for vb in range(VB) for cb in range(CB)]
+            for cb, vb in steps:
+                project(logits[vb][:], vb, piece, cb)
             for vb in range(VB):
                 staged = staging.tile([P, NP], F32, name="staged_half")
                 evacuate(staged[:], logits[vb][:], by_vector=(vb < VB // 2))

@@ -3,8 +3,8 @@ import concourse.mybir as mybir
 P = 128
 C, S, N = 256, 1024, 512
 CB = C // P
-PIECES = 2
-NP = N // PIECES
+FIRST = 3 * N // 8
+PIECES = ((0, FIRST), (FIRST, N - FIRST))
 PARTS = 2
 SP = S // PARTS
 VB = SP // P
@@ -19,85 +19,84 @@ def tile_lumiere1m_kernel(tc, emb, pe, w_out, offs, out):
     nc = tc.nc
     with (
         tc.tile_pool(name="held", bufs=1) as held,
-        tc.tile_pool(name="staging", bufs=PIECES * VB) as staging,
-        tc.psum_pool(name="psum", bufs=VB) as psum,
+        tc.tile_pool(name="staging", bufs=len(PIECES) * VB) as staging,
+        tc.psum_pool(name="psum", bufs=2 * VB) as psum,
     ):
         offsets = held.tile([P, N // 16], U16, name="offsets")
-        nc.sync.dma_start(offsets[:], offs)
 
         table = [held.tile([P, S], F32, name=f"table{cb}") for cb in range(CB)]
-        place = {(cb, piece): held.tile([P, NP], F32, name=f"place{cb}_{piece}")
-                 for cb in range(CB) for piece in range(PIECES)}
+        place = [held.tile([P, N], F32, name=f"place{cb}") for cb in range(CB)]
         weights = {(cb, part): held.tile([P, SP], BF16, name=f"weights{cb}_{part}")
                    for cb in range(CB) for part in range(PARTS)}
 
-        def load_place(cb, piece):
-            nc.sync.dma_start(place[cb, piece][:], pe[cb * P : (cb + 1) * P, piece * NP : (piece + 1) * NP])
+        def load_place(cb, start, width, queue):
+            queue.dma_start(place[cb][:, start : start + width], pe[cb * P : (cb + 1) * P, start : start + width])
 
         def load_weights(cb, part):
             nc.sync.dma_start(weights[cb, part][:], w_out[cb * P : (cb + 1) * P, part * SP : (part + 1) * SP])
 
-        for cb in range(CB):
-            nc.sync.dma_start(table[cb][:], emb[cb * P : (cb + 1) * P, :])
-            load_place(cb, 0)
-        for cb in range(CB):
-            load_place(cb, 1)
-            load_weights(cb, 0)
-        for cb in range(CB):
-            load_weights(cb, 1)
+        load_place(0, 0, N, nc.scalar)
+        load_place(1, *PIECES[0], nc.scalar)
+        nc.sync.dma_start(table[0][:], emb[0:P, :])
+        nc.sync.dma_start(offsets[:], offs)
+        nc.sync.dma_start(table[1][:], emb[P : 2 * P, :])
+        load_place(1, *PIECES[1], nc.sync)
+        for part in range(PARTS):
+            for cb in range(CB):
+                load_weights(cb, part)
 
         zeros = held.tile([P, N], BF16, name="zeros")
         nc.gpsimd.memset(zeros[:], 0.0)
-        unread = psum.tile([P, N], F32, name="unread", tag="half_rows")
+        unread = psum.tile([P, N], F32, name="unread", tag="bank")
         for warmup in range(WARMUPS):
             nc.tensor.matmul(unread[:], zeros[:, 0:P], zeros[:], start=True, stop=True)
 
         hidden = {}
-        for piece in range(PIECES):
-            for cb in range(CB):
-                hidden32 = held.tile([P, NP], F32, name=f"hidden32_{cb}_{piece}")
+        for cb in range(CB):
+            for start, width in PIECES:
+                hidden32 = held.tile([P, width], F32, name=f"hidden32_{cb}_{start}")
                 nc.vector.tensor_tensor(
                     hidden32[:],
-                    table[cb][:].indirect(offsets[:, piece * (NP // 16) : (piece + 1) * (NP // 16)]),
-                    place[cb, piece][:],
+                    table[cb][:].indirect(offsets[:, start // 16 : (start + width) // 16]),
+                    place[cb][:, start : start + width],
                     ADD,
                 )
-                hidden[cb, piece] = held.tile([P, NP], BF16, name=f"hidden{cb}_{piece}")
-                nc.scalar.copy(hidden[cb, piece][:], hidden32[:])
+                hidden[cb, start] = held.tile([P, width], BF16, name=f"hidden{cb}_{start}")
+                nc.scalar.copy(hidden[cb, start][:], hidden32[:])
 
-        def project(logits, vb, piece, cb):
+        def project(logits, part, words, start, cb):
             nc.tensor.matmul(
                 logits,
-                weights[cb, vb // VB][:, (vb % VB) * P : (vb % VB + 1) * P],
-                hidden[cb, piece][:],
+                weights[cb, part][:, words],
+                hidden[cb, start][:],
                 start=(cb == 0),
                 stop=(cb == CB - 1),
             )
 
-        def evacuate(staged, logits, by_vector):
-            if by_vector:
+        def evacuate(staged, logits, block):
+            if block % 2 == 0:
                 nc.vector.tensor_copy(staged, logits)
             else:
                 nc.scalar.copy(staged, logits)
 
-        for piece in range(PIECES):
-            logits = [psum.tile([P, NP], F32, name="half_rows") for vb in range(VB)]
-            steps = [(cb, vb) for cb in range(CB) for vb in range(VB)]
-            if piece > 0:
-                steps = [(cb, vb) for vb in range(VB) for cb in range(CB)]
-            for cb, vb in steps:
-                project(logits[vb][:], vb, piece, cb)
-            for vb in range(VB):
-                staged = staging.tile([P, NP], F32, name="staged_half")
-                evacuate(staged[:], logits[vb][:], by_vector=(vb < VB // 2))
-                nc.sync.dma_start(out[vb * P : (vb + 1) * P, piece * NP : (piece + 1) * NP], staged[:])
+        for start, width in PIECES:
+            logits = [psum.tile([P, width], F32, name="part_rows", tag="bank") for block in range(VB)]
+            for cb in range(CB):
+                for block in range(VB):
+                    project(logits[block][:], 0, slice(block * P, (block + 1) * P), start, cb)
+            for block in range(VB):
+                staged = staging.tile([P, width], F32, name="staged_part")
+                evacuate(staged[:], logits[block][:], block)
+                nc.sync.dma_start(out[block * P : (block + 1) * P, start : start + width], staged[:])
 
-        for vb in range(VB, 2 * VB):
-            staged = staging.tile([P, N], F32, name="staged_whole")
-            for piece in range(PIECES):
-                bank = psum.tile([P, N], F32, name="whole_rows")
-                logits = bank[:, 0:NP]
-                for cb in range(CB):
-                    project(logits, vb, piece, cb)
-                evacuate(staged[:, piece * NP : (piece + 1) * NP], logits, by_vector=(piece == 0))
-            nc.sync.dma_start(out[vb * P : (vb + 1) * P, :], staged[:])
+        for pair in range(VB // 2):
+            staged = staging.tile([P, 2, N], F32, name="staged_pair")
+            for odd in range(2):
+                words = slice(2 * pair * P + odd, 2 * (pair + 1) * P, 2)
+                for start, width in PIECES:
+                    bank = psum.tile([P, width], F32, name="whole_rows", tag="bank")
+                    for cb in range(CB):
+                        project(bank[:], 1, words, start, cb)
+                    evacuate(staged[:, odd, start : start + width], bank[:], odd)
+            rows = out[SP + 2 * pair * P : SP + 2 * (pair + 1) * P, :]
+            nc.sync.dma_start(rows.rearrange("(p k) n -> p k n", k=2), staged[:])

@@ -8,7 +8,8 @@ PIECES = ((0, FIRST), (FIRST, N - FIRST))
 PARTS = 2
 SP = S // PARTS
 VB = SP // P
-WARMUPS = 10
+WARMUPS = 23
+WARM_COLUMNS = 256
 FLOPS = 2 * C * S * N
 
 F32, BF16, U16 = mybir.dt.float32, mybir.dt.bfloat16, mybir.dt.uint16
@@ -45,9 +46,9 @@ def tile_lumiere1m_kernel(tc, emb, pe, w_out, offs, out):
             for cb in range(CB):
                 load_weights(cb, part)
 
-        zeros = held.tile([P, N], BF16, name="zeros")
+        zeros = held.tile([P, WARM_COLUMNS], BF16, name="zeros")
         nc.gpsimd.memset(zeros[:], 0.0)
-        unread = psum.tile([P, N], F32, name="unread", tag="bank")
+        unread = psum.tile([P, WARM_COLUMNS], F32, name="unread", tag="bank")
         for warmup in range(WARMUPS):
             nc.tensor.matmul(unread[:], zeros[:, 0:P], zeros[:], start=True, stop=True)
 
@@ -73,20 +74,20 @@ def tile_lumiere1m_kernel(tc, emb, pe, w_out, offs, out):
                 stop=(cb == CB - 1),
             )
 
-        def evacuate(staged, logits, block):
-            if block % 2 == 0:
+        def evacuate(staged, logits, turn):
+            if turn % 2 == 0:
                 nc.vector.tensor_copy(staged, logits)
             else:
                 nc.scalar.copy(staged, logits)
 
-        for start, width in PIECES:
+        for piece, (start, width) in enumerate(PIECES):
             logits = [psum.tile([P, width], F32, name="part_rows", tag="bank") for block in range(VB)]
             for cb in range(CB):
                 for block in range(VB):
                     project(logits[block][:], 0, slice(block * P, (block + 1) * P), start, cb)
             for block in range(VB):
                 staged = staging.tile([P, width], F32, name="staged_part")
-                evacuate(staged[:], logits[block][:], block)
+                evacuate(staged[:], logits[block][:], piece + block)
                 nc.sync.dma_start(out[block * P : (block + 1) * P, start : start + width], staged[:])
 
         for pair in range(VB // 2):

import concourse.mybir as mybir

P = 128
C, S, N = 256, 1024, 512
CB = C // P
FIRST = 3 * N // 8
PIECES = ((0, FIRST), (FIRST, N - FIRST))
PARTS = 2
SP = S // PARTS
VB = SP // P
WARMUPS = 23
WARM_COLUMNS = 256
FLOPS = 2 * C * S * N

F32, BF16, U16 = mybir.dt.float32, mybir.dt.bfloat16, mybir.dt.uint16
ADD = mybir.AluOpType.add


def tile_lumiere1m_kernel(tc, emb, pe, w_out, offs, out):
    nc = tc.nc
    with (
        tc.tile_pool(name="held", bufs=1) as held,
        tc.tile_pool(name="staging", bufs=len(PIECES) * VB) as staging,
        tc.psum_pool(name="psum", bufs=2 * VB) as psum,
    ):
        offsets = held.tile([P, N // 16], U16, name="offsets")

        table = [held.tile([P, S], F32, name=f"table{cb}") for cb in range(CB)]
        place = [held.tile([P, N], F32, name=f"place{cb}") for cb in range(CB)]
        weights = {(cb, part): held.tile([P, SP], BF16, name=f"weights{cb}_{part}")
                   for cb in range(CB) for part in range(PARTS)}

        def load_place(cb, start, width, queue):
            queue.dma_start(place[cb][:, start : start + width], pe[cb * P : (cb + 1) * P, start : start + width])

        def load_weights(cb, part):
            nc.sync.dma_start(weights[cb, part][:], w_out[cb * P : (cb + 1) * P, part * SP : (part + 1) * SP])

        load_place(0, 0, N, nc.scalar)
        load_place(1, *PIECES[0], nc.scalar)
        nc.sync.dma_start(table[0][:], emb[0:P, :])
        nc.sync.dma_start(offsets[:], offs)
        nc.sync.dma_start(table[1][:], emb[P : 2 * P, :])
        load_place(1, *PIECES[1], nc.sync)
        for part in range(PARTS):
            for cb in range(CB):
                load_weights(cb, part)

        zeros = held.tile([P, WARM_COLUMNS], BF16, name="zeros")
        nc.gpsimd.memset(zeros[:], 0.0)
        unread = psum.tile([P, WARM_COLUMNS], F32, name="unread", tag="bank")
        for warmup in range(WARMUPS):
            nc.tensor.matmul(unread[:], zeros[:, 0:P], zeros[:], start=True, stop=True)

        hidden = {}
        for cb in range(CB):
            for start, width in PIECES:
                hidden32 = held.tile([P, width], F32, name=f"hidden32_{cb}_{start}")
                nc.vector.tensor_tensor(
                    hidden32[:],
                    table[cb][:].indirect(offsets[:, start // 16 : (start + width) // 16]),
                    place[cb][:, start : start + width],
                    ADD,
                )
                hidden[cb, start] = held.tile([P, width], BF16, name=f"hidden{cb}_{start}")
                nc.scalar.copy(hidden[cb, start][:], hidden32[:])

        def project(logits, part, words, start, cb):
            nc.tensor.matmul(
                logits,
                weights[cb, part][:, words],
                hidden[cb, start][:],
                start=(cb == 0),
                stop=(cb == CB - 1),
            )

        def evacuate(staged, logits, turn):
            if turn % 2 == 0:
                nc.vector.tensor_copy(staged, logits)
            else:
                nc.scalar.copy(staged, logits)

        for piece, (start, width) in enumerate(PIECES):
            logits = [psum.tile([P, width], F32, name="part_rows", tag="bank") for block in range(VB)]
            for cb in range(CB):
                for block in range(VB):
                    project(logits[block][:], 0, slice(block * P, (block + 1) * P), start, cb)
            for block in range(VB):
                staged = staging.tile([P, width], F32, name="staged_part")
                evacuate(staged[:], logits[block][:], piece + block)
                nc.sync.dma_start(out[block * P : (block + 1) * P, start : start + width], staged[:])

        for pair in range(VB // 2):
            staged = staging.tile([P, 2, N], F32, name="staged_pair")
            for odd in range(2):
                words = slice(2 * pair * P + odd, 2 * (pair + 1) * P, 2)
                for start, width in PIECES:
                    bank = psum.tile([P, width], F32, name="whole_rows", tag="bank")
                    for cb in range(CB):
                        project(bank[:], 1, words, start, cb)
                    evacuate(staged[:, odd, start : start + width], bank[:], odd)
            rows = out[SP + 2 * pair * P : SP + 2 * (pair + 1) * P, :]
            nc.sync.dma_start(rows.rearrange("(p k) n -> p k n", k=2), staged[:])
